import numpy as np
import ml_dtypes


def mxq(x, axis, fmt="e4m3"):
    dtype, down = {"e4m3": (ml_dtypes.float8_e4m3fn, 7), "e5m2": (ml_dtypes.float8_e5m2, 14)}[fmt]
    v = np.moveaxis(np.asarray(x, np.float32).astype(ml_dtypes.bfloat16).astype(np.float64), axis, -1)
    blocks = v.reshape(v.shape[:-1] + (-1, 32))
    amax = np.abs(blocks).max(-1, keepdims=True)
    byte = np.maximum(np.where(amax > 0, np.frexp(amax)[1] - 1 + 127, 0) - down, 1)
    scale = np.exp2(byte - 127.0)
    codes = (blocks / scale).astype(np.float32).astype(dtype).astype(np.float64)
    return np.moveaxis((codes * scale).reshape(v.shape), -1, axis)


WIDE = False


def mx_kscale(k):
    if not WIDE:
        return np.ones(k)
    levels = np.array([10, -10, 5, -5, 0])
    a = np.random.permutation(np.resize(levels, k // 512 * 4)).reshape(k // 512, 4)
    idx = np.arange(k)
    return np.exp2(a[idx // 512, idx % 128 // 32])


BF16 = ml_dtypes.bfloat16


def bf(x):
    return np.asarray(x, np.float32).astype(BF16)


def f64(x):
    return np.asarray(x).astype(np.float64)


B, S, HID, NH, NOPE, ROPE, VD, KV_RANK, SW, QB = 1, 2048, 1024, 8, 64, 128, 128, 512, 384, 128


def rotate_half(x):
    h = x.shape[-1] // 2
    return np.concatenate([-x[..., h:], x[..., :h]], axis=-1)


def rope_tables():
    pos = np.arange(S, dtype=np.float64)
    inv = 1.0 / (10000.0 ** (np.arange(0, ROPE, 2, dtype=np.float64) / ROPE))
    ang = pos[:, None] * inv[None, :]
    ang = np.concatenate([ang, ang], axis=-1)
    return bf(np.broadcast_to(np.cos(ang)[None], (B, S, ROPE))), bf(np.broadcast_to(np.sin(ang)[None], (B, S, ROPE)))


def setup_inputs():
    s, t = mx_kscale(HID), mx_kscale(KV_RANK)
    col = np.concatenate([t, np.ones(ROPE)])
    cos, sin = rope_tables()
    return {"hidden_states": bf(np.random.standard_normal((B, S, HID)) * s), "cos": cos, "sin": sin,
            "Wkva": bf(np.random.standard_normal((HID, KV_RANK + ROPE)) / np.sqrt(HID) / s[:, None] * col),
            "bkva": bf(np.random.standard_normal(KV_RANK + ROPE) * 0.1 * col),
            "Wkvb": bf(np.random.standard_normal((KV_RANK, NH * (NOPE + VD))) / np.sqrt(KV_RANK) / t[:, None])}


def reference(hidden_states, cos, sin, Wkva, bkva, Wkvb):
    ckv = (mxq(f64(hidden_states), 2, "e4m3") @ mxq(f64(Wkva), 0, "e4m3")) + f64(bkva)
    kv_lat, k_rope = ckv[..., :KV_RANK], ckv[..., KV_RANK:]
    kv = (mxq(kv_lat, 2, "e4m3") @ mxq(f64(Wkvb), 0, "e4m3")).reshape(B, S, NH, NOPE + VD).transpose(0, 2, 1, 3)
    k_nope, v = kv[..., :NOPE], kv[..., NOPE:]
    k_rope = k_rope.reshape(B, 1, S, ROPE)
    c, si = f64(cos)[:, None], f64(sin)[:, None]
    k_rope = k_rope * c + rotate_half(k_rope) * si
    k_rope = np.broadcast_to(k_rope, (B, NH, S, ROPE))
    kk = np.concatenate([k_nope, k_rope], axis=-1)
    return kk, np.ascontiguousarray(v)

@@ -1,0 +1,272 @@
+from contextlib import ExitStack
+
+import concourse.mybir as mybir
+from concourse.masks import make_identity
+
+F32 = mybir.dt.float32
+BF16 = mybir.dt.bfloat16
+U32 = mybir.dt.uint32
+U8 = mybir.dt.uint8
+FP8X4 = mybir.dt.float8_e4m3fn_x4
+ADD = mybir.AluOpType.add
+MULT = mybir.AluOpType.mult
+
+P = 128
+PACK = 4
+K_PASS = P * PACK
+
+SEQ = 2048
+HID = 1024
+HEADS = 8
+NOPE = 64
+ROPE = 128
+VDIM = 128
+RANK = 512
+
+HID_PASSES = HID // K_PASS
+WORD_BLOCKS = HID // 2 // P
+TILES_PER_GROUP = 4
+GROUPS = SEQ // (P * TILES_PER_GROUP)
+HALF_HEADS = HEADS // 2
+HALF_ROPE = ROPE // 2
+KV_CHUNK = 512
+BIAS_ROWS = (RANK + ROPE) // P
+
+FLOPS = 2 * SEQ * HID * (RANK + ROPE) + 2 * SEQ * RANK * HEADS * (NOPE + VDIM)
+
+
+def tile_gptossmlaattention_pa_kernel(tc, hidden_states, cos, sin, Wkva, bkva, Wkvb, out_0, out_1):
+    nc = tc.nc
+    J = TILES_PER_GROUP
+
+    hid_dram = hidden_states[0, :, :].rearrange("(g p j) k -> g p (j k)", p=P, j=J)
+    cos_dram = cos[0, :, :].rearrange("(g p j) d -> p g (j d)", p=P, j=J)
+    sin_dram = sin[0, :, :].rearrange("(g p j) d -> p g (j d)", p=P, j=J)
+    kk_dram = out_0[0, :, :, :].rearrange("h (g p j) d -> g p h (j d)", p=P, j=J)
+    v_dram = out_1[0, :, :, :].rearrange("h (g p j) d -> g p h (j d)", p=P, j=J)
+    wa_dram = Wkva.rearrange("(kp u p e) c -> kp p u (e c)", kp=HID_PASSES, u=2, p=P, e=2)
+    wb_dram = Wkvb.rearrange("(t p) n -> p t n", p=P)
+
+    with ExitStack() as ctx:
+        const = ctx.enter_context(tc.tile_pool(name="const", bufs=1))
+        inputs = ctx.enter_context(tc.tile_pool(name="inputs", bufs=1))
+        wstage = ctx.enter_context(tc.tile_pool(name="wstage", bufs=2))
+        work = ctx.enter_context(tc.tile_pool(name="work", bufs=3))
+        rope_pool = ctx.enter_context(tc.tile_pool(name="rope", bufs=2))
+        kk_pool = ctx.enter_context(tc.tile_pool(name="kk", bufs=2))
+        v_pool = ctx.enter_context(tc.tile_pool(name="v", bufs=6))
+        psum_xt = ctx.enter_context(tc.psum_pool(name="psum_xt", bufs=2))
+        psum_lat = ctx.enter_context(tc.psum_pool(name="psum_lat", bufs=2))
+        psum_rope = ctx.enter_context(tc.psum_pool(name="psum_rope", bufs=1))
+        psum_kv = ctx.enter_context(tc.psum_pool(name="psum_kv", bufs=3))
+
+        bias_rows = const.tile([P, P], BF16)
+        nc.vector.memset(bias_rows[:], 0.0)
+        nc.scalar.dma_start(out=bias_rows[0:BIAS_ROWS, :], in_=bkva.rearrange("(r c) -> r c", c=P))
+
+        raw_a = inputs.tile([P, HID_PASSES, PACK, RANK + ROPE], BF16)
+        for kp in range(HID_PASSES):
+            nc.sync.dma_start(
+                out=raw_a[:, kp, :, :].rearrange("p (u e) c -> p u (e c)", e=2), in_=wa_dram[kp]
+            )
+        hid_raw = [inputs.tile([P, J * HID], BF16, name="hid_raw%d" % g) for g in range(GROUPS)]
+        nc.sync.dma_start(out=hid_raw[0][:], in_=hid_dram[0])
+        raw_b = inputs.tile([P, PACK, HEADS * (NOPE + VDIM)], BF16)
+        half_cols = HALF_HEADS * (NOPE + VDIM)
+        for half in range(2):
+            cols = slice(half * half_cols, (half + 1) * half_cols)
+            nc.sync.dma_start(out=raw_b[:, :, cols], in_=wb_dram[:, :, cols])
+        cos_sb = inputs.tile([P, GROUPS, J * ROPE], BF16)
+        sin_sb = inputs.tile([P, GROUPS, J * ROPE], BF16)
+        nc.sync.dma_start(out=cos_sb[:], in_=cos_dram)
+        nc.sync.dma_start(out=sin_sb[:], in_=sin_dram)
+        for g in range(1, GROUPS):
+            nc.sync.dma_start(out=hid_raw[g][:], in_=hid_dram[g])
+
+        ident_f32 = const.tile([P, P], F32)
+        make_identity(nc, ident_f32[:])
+        ident_bf16 = const.tile([P, P], BF16)
+        nc.vector.tensor_copy(out=ident_bf16[:], in_=ident_f32[:])
+
+        bias_t_ps = psum_xt.tile([P, P], BF16, tag="xt")
+        nc.tensor.transpose(out=bias_t_ps[:], in_=bias_rows[:], identity=ident_bf16[:])
+        lat_bias = const.tile([P, PACK], F32)
+        nc.vector.tensor_copy(out=lat_bias[:], in_=bias_t_ps[:, 0:PACK])
+        rope_bias_ps = psum_xt.tile([P, ROPE], F32, tag="xt")
+        nc.tensor.matmul(
+            out=rope_bias_ps[:],
+            lhsT=ident_bf16[:, BIAS_ROWS - 1 : BIAS_ROWS].to_broadcast([P, P]),
+            rhs=bias_rows[:],
+            start=True,
+            stop=True,
+        )
+        rope_bias = const.tile([P, ROPE], F32)
+        nc.vector.tensor_copy(out=rope_bias[:], in_=rope_bias_ps[:])
+
+        a_codes = const.tile([P, HID_PASSES, RANK + ROPE], U32, align_bytes=64)
+        a_scales = const.tile([P, HID_PASSES, RANK + ROPE], U8, align_bytes=64)
+        grouped_a = []
+        for kp in range(HID_PASSES):
+            grouped = wstage.tile([P, RANK + ROPE, PACK], BF16, align_bytes=64, name="grouped_a", tag="grouped_a")
+            nc.vector.tensor_copy(
+                out=grouped[:].rearrange("p (c i) t -> p c t i", i=4),
+                in_=raw_a[:, kp, :, :].rearrange("p t (c i) -> p c t i", i=4),
+            )
+            grouped_a.append(grouped)
+        for kp in range(HID_PASSES):
+            for cols in (slice(0, RANK), slice(RANK, RANK + ROPE)):
+                nc.vector.quantize_mx(
+                    out=a_codes[:, kp, cols].bitcast(FP8X4),
+                    scales=a_scales[:, kp, cols],
+                    in_=grouped_a[kp][:, cols, :].rearrange("p c t -> p (c t)"),
+                )
+
+        b_codes = const.tile([P, 3 * KV_CHUNK], U32, align_bytes=64)
+        b_scales = const.tile([P, 3 * KV_CHUNK], U8, align_bytes=64)
+        raw_b_heads = raw_b[:].rearrange("p t (h x) -> p t h x", x=NOPE + VDIM)
+        b_sources = [
+            raw_b_heads[:, :, 0:HALF_HEADS, NOPE:],
+            raw_b_heads[:, :, HALF_HEADS:HEADS, NOPE:],
+            raw_b_heads[:, :, :, 0:NOPE],
+        ]
+        for n in range(3):
+            grouped = wstage.tile([P, KV_CHUNK, PACK], BF16, align_bytes=64, name="grouped_b", tag="grouped_b")
+            copy = nc.vector.tensor_copy if n == 2 else nc.scalar.copy
+            copy(
+                out=grouped[:].rearrange("p (h d) t -> p h d t", h=b_sources[n].shape[2]),
+                in_=b_sources[n].rearrange("p t h d -> p h d t"),
+            )
+            cols = slice(n * KV_CHUNK, (n + 1) * KV_CHUNK)
+            nc.vector.quantize_mx(
+                out=b_codes[:, cols].bitcast(FP8X4),
+                scales=b_scales[:, cols],
+                in_=grouped[:].rearrange("p c t -> p (c t)"),
+            )
+
+        for g in range(GROUPS):
+            hid_words = hid_raw[g][:].bitcast(F32)
+            rope_ps = psum_rope.tile([P, J, ROPE], F32)
+            kk_stage = kk_pool.tile([P, HEADS, J, NOPE + ROPE], F32)
+            v_stage = [
+                v_pool.tile([P, HALF_HEADS, J, VDIM], F32, name="v_stage", tag="v_stage") for half in range(2)
+            ]
+
+            for j in range(J):
+                xt = psum_xt.tile([P, WORD_BLOCKS, P], F32, tag="xt")
+                for q in range(WORD_BLOCKS):
+                    w0 = (j * WORD_BLOCKS + q) * P
+                    nc.tensor.transpose(out=xt[:, q, :], in_=hid_words[:, w0 : w0 + P], identity=ident_f32[:])
+                hid_grouped = work.tile([P, HID_PASSES * P * PACK], BF16, align_bytes=64)
+                nc.scalar.copy(
+                    out=hid_grouped[:].bitcast(F32).rearrange("p (kp c u) -> p kp c u", kp=HID_PASSES, u=2),
+                    in_=xt[:].rearrange("p (kp u) c -> p kp c u", u=2),
+                )
+                hid_codes = work.tile([P, HID_PASSES, P], U32, align_bytes=64)
+                hid_scales = work.tile([P, HID_PASSES, P], U8, align_bytes=64)
+                nc.vector.quantize_mx(
+                    out=hid_codes[:].rearrange("p kp c -> p (kp c)").bitcast(FP8X4),
+                    scales=hid_scales[:].rearrange("p kp c -> p (kp c)"),
+                    in_=hid_grouped[:],
+                )
+
+                lat_ps = psum_lat.tile([P, PACK, P], F32)
+                for t in range(PACK):
+                    for kp in range(HID_PASSES):
+                        nc.tensor.matmul_mx(
+                            out=lat_ps[:, t, :],
+                            lhsT=a_codes[:, kp, t * P : (t + 1) * P].bitcast(FP8X4),
+                            lhsT_scale=a_scales[:, kp, t * P : (t + 1) * P],
+                            rhs=hid_codes[:, kp, :].bitcast(FP8X4),
+                            rhs_scale=hid_scales[:, kp, :],
+                            start=(kp == 0),
+                            stop=(kp == HID_PASSES - 1),
+                        )
+                for kp in range(HID_PASSES):
+                    nc.tensor.matmul_mx(
+                        out=rope_ps[:, j, :],
+                        lhsT=hid_codes[:, kp, :].bitcast(FP8X4),
+                        lhsT_scale=hid_scales[:, kp, :],
+                        rhs=a_codes[:, kp, RANK : RANK + ROPE].bitcast(FP8X4),
+                        rhs_scale=a_scales[:, kp, RANK : RANK + ROPE],
+                        start=(kp == 0),
+                        stop=(kp == HID_PASSES - 1),
+                    )
+
+                lat_grouped = work.tile([P, P, PACK], BF16, align_bytes=64)
+                nc.vector.tensor_tensor(
+                    out=lat_grouped[:],
+                    in0=lat_ps[:].rearrange("p t c -> p c t"),
+                    in1=lat_bias[:].unsqueeze(1).to_broadcast([P, P, PACK]),
+                    op=ADD,
+                )
+                lat_codes = work.tile([P, P], U32, align_bytes=64)
+                lat_scales = work.tile([P, P], U8, align_bytes=64)
+                nc.vector.quantize_mx(
+                    out=lat_codes[:].bitcast(FP8X4),
+                    scales=lat_scales[:],
+                    in_=lat_grouped[:].rearrange("p c t -> p (c t)"),
+                )
+
+                for n in range(3):
+                    kv_ps = psum_kv.tile([P, KV_CHUNK], F32)
+                    cols = slice(n * KV_CHUNK, (n + 1) * KV_CHUNK)
+                    nc.tensor.matmul_mx(
+                        out=kv_ps[:],
+                        lhsT=lat_codes[:].bitcast(FP8X4),
+                        lhsT_scale=lat_scales[:],
+                        rhs=b_codes[:, cols].bitcast(FP8X4),
+                        rhs_scale=b_scales[:, cols],
+                        start=True,
+                        stop=True,
+                    )
+                    if n < 2:
+                        nc.scalar.copy(
+                            out=v_stage[n][:, :, j, :], in_=kv_ps[:].rearrange("p (h d) -> p h d", d=VDIM)
+                        )
+                    else:
+                        nc.scalar.copy(
+                            out=kk_stage[:, :, j, 0:NOPE], in_=kv_ps[:].rearrange("p (h d) -> p h d", d=NOPE)
+                        )
+
+            for half in range(2):
+                heads = slice(half * HALF_HEADS, (half + 1) * HALF_HEADS)
+                nc.sync.dma_start(
+                    out=v_dram[g, :, heads, :], in_=v_stage[half][:].rearrange("p h j d -> p h (j d)")
+                )
+
+            cos_g = cos_sb[:, g, :].rearrange("p (j d) -> p j d", d=ROPE)
+            sin_g = sin_sb[:, g, :].rearrange("p (j d) -> p j d", d=ROPE)
+            k_rope = rope_pool.tile([P, J, ROPE], F32)
+            nc.vector.tensor_tensor(
+                out=k_rope[:],
+                in0=rope_ps[:],
+                in1=rope_bias[:].unsqueeze(1).to_broadcast([P, J, ROPE]),
+                op=ADD,
+            )
+            k_rot = rope_pool.tile([P, J, ROPE], F32)
+            nc.vector.tensor_tensor(out=k_rot[:], in0=k_rope[:], in1=cos_g, op=MULT)
+            crossed = rope_pool.tile([P, J, ROPE], F32)
+            nc.vector.scalar_tensor_tensor(
+                out=crossed[:, :, 0:HALF_ROPE],
+                in0=k_rope[:, :, HALF_ROPE:ROPE],
+                scalar=-1.0,
+                in1=sin_g[:, :, 0:HALF_ROPE],
+                op0=MULT,
+                op1=MULT,
+            )
+            nc.vector.tensor_tensor(
+                out=crossed[:, :, HALF_ROPE:ROPE],
+                in0=k_rope[:, :, 0:HALF_ROPE],
+                in1=sin_g[:, :, HALF_ROPE:ROPE],
+                op=MULT,
+            )
+            nc.vector.tensor_tensor(out=k_rot[:], in0=k_rot[:], in1=crossed[:], op=ADD)
+            for half in range(2):
+                heads = slice(half * HALF_HEADS, (half + 1) * HALF_HEADS)
+                nc.vector.tensor_copy(
+                    out=kk_stage[:, heads, :, NOPE:],
+                    in_=k_rot[:].unsqueeze(1).to_broadcast([P, HALF_HEADS, J, ROPE]),
+                )
+                nc.sync.dma_start(
+                    out=kk_dram[g, :, heads, :], in_=kk_stage[:, heads, :, :].rearrange("p h j d -> p h (j d)")
+                )

@@ -25,25 +25,28 @@ RANK = 512
 
 HID_PASSES = HID // K_PASS
 WORD_BLOCKS = HID // 2 // P
-TILES_PER_GROUP = 4
-GROUPS = SEQ // (P * TILES_PER_GROUP)
+J = 4
+GROUPS = SEQ // (P * J)
+TILES = GROUPS * J
 HALF_HEADS = HEADS // 2
 HALF_ROPE = ROPE // 2
 KV_CHUNK = 512
+KV_CHUNKS = HEADS * (NOPE + VDIM) // KV_CHUNK
 BIAS_ROWS = (RANK + ROPE) // P
+
+GROUP_LAG = J
 
 FLOPS = 2 * SEQ * HID * (RANK + ROPE) + 2 * SEQ * RANK * HEADS * (NOPE + VDIM)
 
 
 def tile_gptossmlaattention_pa_kernel(tc, hidden_states, cos, sin, Wkva, bkva, Wkvb, out_0, out_1):
     nc = tc.nc
-    J = TILES_PER_GROUP
 
-    hid_dram = hidden_states[0, :, :].rearrange("(g p j) k -> g p (j k)", p=P, j=J)
-    cos_dram = cos[0, :, :].rearrange("(g p j) d -> p g (j d)", p=P, j=J)
-    sin_dram = sin[0, :, :].rearrange("(g p j) d -> p g (j d)", p=P, j=J)
-    kk_dram = out_0[0, :, :, :].rearrange("h (g p j) d -> g p h (j d)", p=P, j=J)
-    v_dram = out_1[0, :, :, :].rearrange("h (g p j) d -> g p h (j d)", p=P, j=J)
+    hid_dram = hidden_states[0, :, :].rearrange("(p g j) k -> g p (j k)", p=P, j=J)
+    cos_dram = cos[0, :, :].rearrange("(p s) d -> p (s d)", p=P)
+    sin_dram = sin[0, :, :].rearrange("(p s) d -> p (s d)", p=P)
+    kk_dram = out_0[0, :, :, :].rearrange("h (p g j) d -> g p h (j d)", p=P, j=J)
+    v_dram = out_1[0, :, :, :].rearrange("h (p g j) d -> g p h (j d)", p=P, j=J)
     wa_dram = Wkva.rearrange("(kp u p e) c -> kp p u (e c)", kp=HID_PASSES, u=2, p=P, e=2)
     wb_dram = Wkvb.rearrange("(t p) n -> p t n", p=P)
 
@@ -76,11 +79,12 @@ def tile_gptossmlaattention_pa_kernel(tc, hidden_states, cos, sin, Wkva, bkva, W
         for half in range(2):
             cols = slice(half * half_cols, (half + 1) * half_cols)
             nc.sync.dma_start(out=raw_b[:, :, cols], in_=wb_dram[:, :, cols])
-        cos_sb = inputs.tile([P, GROUPS, J * ROPE], BF16)
-        sin_sb = inputs.tile([P, GROUPS, J * ROPE], BF16)
-        nc.sync.dma_start(out=cos_sb[:], in_=cos_dram)
-        nc.sync.dma_start(out=sin_sb[:], in_=sin_dram)
-        for g in range(1, GROUPS):
+        nc.sync.dma_start(out=hid_raw[1][:], in_=hid_dram[1])
+        cos_sb = inputs.tile([P, GROUPS, J, ROPE], BF16)
+        sin_sb = inputs.tile([P, GROUPS, J, ROPE], BF16)
+        nc.sync.dma_start(out=cos_sb[:].rearrange("p g j d -> p (g j d)"), in_=cos_dram)
+        nc.sync.dma_start(out=sin_sb[:].rearrange("p g j d -> p (g j d)"), in_=sin_dram)
+        for g in range(2, GROUPS):
             nc.sync.dma_start(out=hid_raw[g][:], in_=hid_dram[g])
 
         ident_f32 = const.tile([P, P], F32)
@@ -121,152 +125,186 @@ def tile_gptossmlaattention_pa_kernel(tc, hidden_states, cos, sin, Wkva, bkva, W
                     in_=grouped_a[kp][:, cols, :].rearrange("p c t -> p (c t)"),
                 )
 
-        b_codes = const.tile([P, 3 * KV_CHUNK], U32, align_bytes=64)
-        b_scales = const.tile([P, 3 * KV_CHUNK], U8, align_bytes=64)
+        b_codes = const.tile([P, KV_CHUNKS * KV_CHUNK], U32, align_bytes=64)
+        b_scales = const.tile([P, KV_CHUNKS * KV_CHUNK], U8, align_bytes=64)
         raw_b_heads = raw_b[:].rearrange("p t (h x) -> p t h x", x=NOPE + VDIM)
         b_sources = [
             raw_b_heads[:, :, 0:HALF_HEADS, NOPE:],
             raw_b_heads[:, :, HALF_HEADS:HEADS, NOPE:],
             raw_b_heads[:, :, :, 0:NOPE],
         ]
-        for n in range(3):
-            grouped = wstage.tile([P, KV_CHUNK, PACK], BF16, align_bytes=64, name="grouped_b", tag="grouped_b")
-            copy = nc.vector.tensor_copy if n == 2 else nc.scalar.copy
+        grouped_b = {}
+
+        def regroup_b(n):
+            grouped_b[n] = wstage.tile([P, KV_CHUNK, PACK], BF16, align_bytes=64, name="grouped_b", tag="grouped_b")
+            copy = nc.scalar.copy if n < 2 else nc.vector.tensor_copy
             copy(
-                out=grouped[:].rearrange("p (h d) t -> p h d t", h=b_sources[n].shape[2]),
+                out=grouped_b[n][:].rearrange("p (h d) t -> p h d t", h=b_sources[n].shape[2]),
                 in_=b_sources[n].rearrange("p t h d -> p h d t"),
             )
+
+        def quantise_b(n):
             cols = slice(n * KV_CHUNK, (n + 1) * KV_CHUNK)
             nc.vector.quantize_mx(
                 out=b_codes[:, cols].bitcast(FP8X4),
                 scales=b_scales[:, cols],
-                in_=grouped[:].rearrange("p c t -> p (c t)"),
+                in_=grouped_b[n][:].rearrange("p c t -> p (c t)"),
             )
 
-        for g in range(GROUPS):
+        hid_q = {}
+        lat_q = {}
+        rope_ps = {}
+        rope_sb = {}
+        kk_stage = {}
+        v_stage = {}
+
+        def front(i):
+            g, j = divmod(i, J)
             hid_words = hid_raw[g][:].bitcast(F32)
-            rope_ps = psum_rope.tile([P, J, ROPE], F32)
-            kk_stage = kk_pool.tile([P, HEADS, J, NOPE + ROPE], F32)
-            v_stage = [
-                v_pool.tile([P, HALF_HEADS, J, VDIM], F32, name="v_stage", tag="v_stage") for half in range(2)
-            ]
+            xt = psum_xt.tile([P, WORD_BLOCKS, P], F32, tag="xt")
+            for q in range(WORD_BLOCKS):
+                w0 = (j * WORD_BLOCKS + q) * P
+                nc.tensor.transpose(out=xt[:, q, :], in_=hid_words[:, w0 : w0 + P], identity=ident_f32[:])
+            hid_grouped = work.tile([P, HID_PASSES * P * PACK], BF16, align_bytes=64)
+            nc.scalar.copy(
+                out=hid_grouped[:].bitcast(F32).rearrange("p (kp c u) -> p kp c u", kp=HID_PASSES, u=2),
+                in_=xt[:].rearrange("p (kp u) c -> p kp c u", u=2),
+            )
+            hid_codes = work.tile([P, HID_PASSES, P], U32, align_bytes=64)
+            hid_scales = work.tile([P, HID_PASSES, P], U8, align_bytes=64)
+            nc.vector.quantize_mx(
+                out=hid_codes[:].rearrange("p kp c -> p (kp c)").bitcast(FP8X4),
+                scales=hid_scales[:].rearrange("p kp c -> p (kp c)"),
+                in_=hid_grouped[:],
+            )
+            hid_q[i] = (hid_codes, hid_scales)
 
-            for j in range(J):
-                xt = psum_xt.tile([P, WORD_BLOCKS, P], F32, tag="xt")
-                for q in range(WORD_BLOCKS):
-                    w0 = (j * WORD_BLOCKS + q) * P
-                    nc.tensor.transpose(out=xt[:, q, :], in_=hid_words[:, w0 : w0 + P], identity=ident_f32[:])
-                hid_grouped = work.tile([P, HID_PASSES * P * PACK], BF16, align_bytes=64)
-                nc.scalar.copy(
-                    out=hid_grouped[:].bitcast(F32).rearrange("p (kp c u) -> p kp c u", kp=HID_PASSES, u=2),
-                    in_=xt[:].rearrange("p (kp u) c -> p kp c u", u=2),
+        def middle(i):
+            g, j = divmod(i, J)
+            hid_codes, hid_scales = hid_q[i]
+            if j == 0:
+                rope_ps[g] = psum_rope.tile([P, J, ROPE], F32, name="rope_ps")
+                lat_q[g] = (
+                    work.tile([P, J, P], U32, align_bytes=64, name="lat_codes"),
+                    work.tile([P, J, P], U8, align_bytes=64, name="lat_scales"),
                 )
-                hid_codes = work.tile([P, HID_PASSES, P], U32, align_bytes=64)
-                hid_scales = work.tile([P, HID_PASSES, P], U8, align_bytes=64)
-                nc.vector.quantize_mx(
-                    out=hid_codes[:].rearrange("p kp c -> p (kp c)").bitcast(FP8X4),
-                    scales=hid_scales[:].rearrange("p kp c -> p (kp c)"),
-                    in_=hid_grouped[:],
-                )
-
-                lat_ps = psum_lat.tile([P, PACK, P], F32)
-                for t in range(PACK):
-                    for kp in range(HID_PASSES):
-                        nc.tensor.matmul_mx(
-                            out=lat_ps[:, t, :],
-                            lhsT=a_codes[:, kp, t * P : (t + 1) * P].bitcast(FP8X4),
-                            lhsT_scale=a_scales[:, kp, t * P : (t + 1) * P],
-                            rhs=hid_codes[:, kp, :].bitcast(FP8X4),
-                            rhs_scale=hid_scales[:, kp, :],
-                            start=(kp == 0),
-                            stop=(kp == HID_PASSES - 1),
-                        )
+            lat_ps = psum_lat.tile([P, PACK, P], F32)
+            for t in range(PACK):
                 for kp in range(HID_PASSES):
                     nc.tensor.matmul_mx(
-                        out=rope_ps[:, j, :],
-                        lhsT=hid_codes[:, kp, :].bitcast(FP8X4),
-                        lhsT_scale=hid_scales[:, kp, :],
-                        rhs=a_codes[:, kp, RANK : RANK + ROPE].bitcast(FP8X4),
-                        rhs_scale=a_scales[:, kp, RANK : RANK + ROPE],
+                        out=lat_ps[:, t, :],
+                        lhsT=a_codes[:, kp, t * P : (t + 1) * P].bitcast(FP8X4),
+                        lhsT_scale=a_scales[:, kp, t * P : (t + 1) * P],
+                        rhs=hid_codes[:, kp, :].bitcast(FP8X4),
+                        rhs_scale=hid_scales[:, kp, :],
                         start=(kp == 0),
                         stop=(kp == HID_PASSES - 1),
                     )
-
-                lat_grouped = work.tile([P, P, PACK], BF16, align_bytes=64)
-                nc.vector.tensor_tensor(
-                    out=lat_grouped[:],
-                    in0=lat_ps[:].rearrange("p t c -> p c t"),
-                    in1=lat_bias[:].unsqueeze(1).to_broadcast([P, P, PACK]),
-                    op=ADD,
+            for kp in range(HID_PASSES):
+                nc.tensor.matmul_mx(
+                    out=rope_ps[g][:, j, :],
+                    lhsT=hid_codes[:, kp, :].bitcast(FP8X4),
+                    lhsT_scale=hid_scales[:, kp, :],
+                    rhs=a_codes[:, kp, RANK : RANK + ROPE].bitcast(FP8X4),
+                    rhs_scale=a_scales[:, kp, RANK : RANK + ROPE],
+                    start=(kp == 0),
+                    stop=(kp == HID_PASSES - 1),
                 )
-                lat_codes = work.tile([P, P], U32, align_bytes=64)
-                lat_scales = work.tile([P, P], U8, align_bytes=64)
-                nc.vector.quantize_mx(
-                    out=lat_codes[:].bitcast(FP8X4),
-                    scales=lat_scales[:],
-                    in_=lat_grouped[:].rearrange("p c t -> p (c t)"),
-                )
-
-                for n in range(3):
-                    kv_ps = psum_kv.tile([P, KV_CHUNK], F32)
-                    cols = slice(n * KV_CHUNK, (n + 1) * KV_CHUNK)
-                    nc.tensor.matmul_mx(
-                        out=kv_ps[:],
-                        lhsT=lat_codes[:].bitcast(FP8X4),
-                        lhsT_scale=lat_scales[:],
-                        rhs=b_codes[:, cols].bitcast(FP8X4),
-                        rhs_scale=b_scales[:, cols],
-                        start=True,
-                        stop=True,
-                    )
-                    if n < 2:
-                        nc.scalar.copy(
-                            out=v_stage[n][:, :, j, :], in_=kv_ps[:].rearrange("p (h d) -> p h d", d=VDIM)
-                        )
-                    else:
-                        nc.scalar.copy(
-                            out=kk_stage[:, :, j, 0:NOPE], in_=kv_ps[:].rearrange("p (h d) -> p h d", d=NOPE)
-                        )
-
-            for half in range(2):
-                heads = slice(half * HALF_HEADS, (half + 1) * HALF_HEADS)
-                nc.sync.dma_start(
-                    out=v_dram[g, :, heads, :], in_=v_stage[half][:].rearrange("p h j d -> p h (j d)")
-                )
-
-            cos_g = cos_sb[:, g, :].rearrange("p (j d) -> p j d", d=ROPE)
-            sin_g = sin_sb[:, g, :].rearrange("p (j d) -> p j d", d=ROPE)
-            k_rope = rope_pool.tile([P, J, ROPE], F32)
+            lat_grouped = work.tile([P, P, PACK], BF16, align_bytes=64)
             nc.vector.tensor_tensor(
-                out=k_rope[:],
-                in0=rope_ps[:],
-                in1=rope_bias[:].unsqueeze(1).to_broadcast([P, J, ROPE]),
+                out=lat_grouped[:],
+                in0=lat_ps[:].rearrange("p t c -> p c t"),
+                in1=lat_bias[:].unsqueeze(1).to_broadcast([P, P, PACK]),
                 op=ADD,
             )
-            k_rot = rope_pool.tile([P, J, ROPE], F32)
-            nc.vector.tensor_tensor(out=k_rot[:], in0=k_rope[:], in1=cos_g, op=MULT)
-            crossed = rope_pool.tile([P, J, ROPE], F32)
-            nc.vector.scalar_tensor_tensor(
-                out=crossed[:, :, 0:HALF_ROPE],
-                in0=k_rope[:, :, HALF_ROPE:ROPE],
-                scalar=-1.0,
-                in1=sin_g[:, :, 0:HALF_ROPE],
-                op0=MULT,
-                op1=MULT,
+            lat_codes, lat_scales = lat_q[g]
+            nc.vector.quantize_mx(
+                out=lat_codes[:, j, :].bitcast(FP8X4),
+                scales=lat_scales[:, j, :],
+                in_=lat_grouped[:].rearrange("p c t -> p (c t)"),
             )
-            nc.vector.tensor_tensor(
-                out=crossed[:, :, HALF_ROPE:ROPE],
-                in0=k_rope[:, :, 0:HALF_ROPE],
-                in1=sin_g[:, :, HALF_ROPE:ROPE],
-                op=MULT,
-            )
-            nc.vector.tensor_tensor(out=k_rot[:], in0=k_rot[:], in1=crossed[:], op=ADD)
-            for half in range(2):
-                heads = slice(half * HALF_HEADS, (half + 1) * HALF_HEADS)
+
+        def rotate(g, part):
+            if part == 0:
+                kk_stage[g] = kk_pool.tile([P, HEADS, J, NOPE + ROPE], F32, name="kk_stage")
+                rope_sb[g] = (
+                    rope_pool.tile([P, J, ROPE], F32, name="k_rope"),
+                    rope_pool.tile([P, J, ROPE], F32, name="k_rot"),
+                    rope_pool.tile([P, J, ROPE], F32, name="crossed"),
+                )
+            k_rope, k_rot, crossed = rope_sb[g]
+            lo = slice(0, HALF_ROPE)
+            hi = slice(HALF_ROPE, ROPE)
+            if part == 0:
+                nc.vector.tensor_tensor(
+                    out=k_rope[:],
+                    in0=rope_ps[g][:],
+                    in1=rope_bias[:].unsqueeze(1).to_broadcast([P, J, ROPE]),
+                    op=ADD,
+                )
+            if part == 1:
+                nc.vector.tensor_tensor(out=k_rot[:], in0=k_rope[:], in1=cos_sb[:, g, :, :], op=MULT)
+                nc.vector.scalar_tensor_tensor(
+                    out=crossed[:, :, lo], in0=k_rope[:, :, hi], scalar=-1.0, in1=sin_sb[:, g, :, lo], op0=MULT, op1=MULT
+                )
+                nc.vector.tensor_tensor(out=crossed[:, :, hi], in0=k_rope[:, :, lo], in1=sin_sb[:, g, :, hi], op=MULT)
+            if part == 2:
+                nc.vector.tensor_tensor(out=k_rot[:], in0=k_rot[:], in1=crossed[:], op=ADD)
+            if part >= 2:
+                heads = slice((part - 2) * HALF_HEADS, (part - 1) * HALF_HEADS)
                 nc.vector.tensor_copy(
-                    out=kk_stage[:, heads, :, NOPE:],
+                    out=kk_stage[g][:, heads, :, NOPE:],
                     in_=k_rot[:].unsqueeze(1).to_broadcast([P, HALF_HEADS, J, ROPE]),
                 )
+
+        def second(g, n, j):
+            if n == 0 and j == 0:
+                v_stage[g] = [
+                    v_pool.tile([P, HALF_HEADS, J, VDIM], F32, name="v_stage", tag="v_stage") for half in range(2)
+                ]
+            lat_codes, lat_scales = lat_q[g]
+            kv_ps = psum_kv.tile([P, KV_CHUNK], F32)
+            cols = slice(n * KV_CHUNK, (n + 1) * KV_CHUNK)
+            nc.tensor.matmul_mx(
+                out=kv_ps[:],
+                lhsT=lat_codes[:, j, :].bitcast(FP8X4),
+                lhsT_scale=lat_scales[:, j, :],
+                rhs=b_codes[:, cols].bitcast(FP8X4),
+                rhs_scale=b_scales[:, cols],
+                start=True,
+                stop=True,
+            )
+            if n < 2:
+                nc.scalar.copy(out=v_stage[g][n][:, :, j, :], in_=kv_ps[:].rearrange("p (h d) -> p h d", d=VDIM))
+                if j == J - 1:
+                    heads = slice(n * HALF_HEADS, (n + 1) * HALF_HEADS)
+                    nc.sync.dma_start(
+                        out=v_dram[g, :, heads, :], in_=v_stage[g][n][:].rearrange("p h j d -> p h (j d)")
+                    )
+            else:
+                nc.scalar.copy(out=kk_stage[g][:, :, j, 0:NOPE], in_=kv_ps[:].rearrange("p (h d) -> p h d", d=NOPE))
+
+        def store_kk(g):
+            for half in range(2):
+                heads = slice(half * HALF_HEADS, (half + 1) * HALF_HEADS)
                 nc.sync.dma_start(
-                    out=kk_dram[g, :, heads, :], in_=kk_stage[:, heads, :, :].rearrange("p h j d -> p h (j d)")
+                    out=kk_dram[g, :, heads, :], in_=kk_stage[g][:, heads, :, :].rearrange("p h j d -> p h (j d)")
                 )
+
+        for s in range(TILES + GROUP_LAG):
+            if s % 2 == 0 and 1 <= s // 2 <= KV_CHUNKS:
+                quantise_b(s // 2 - 1)
+            if s >= GROUP_LAG:
+                g, quarter = divmod(s - GROUP_LAG, J)
+                for unit in range(KV_CHUNKS * quarter, KV_CHUNKS * (quarter + 1)):
+                    second(g, *divmod(unit, J))
+            if s < TILES:
+                front(s)
+            if s % 2 == 1 and s // 2 < KV_CHUNKS:
+                regroup_b(s // 2)
+            if 1 <= s <= TILES:
+                middle(s - 1)
+            if s >= GROUP_LAG:
+                rotate(g, quarter)
+                if quarter == J - 1:
+                    store_kk(g)

@@ -58,10 +58,9 @@ def tile_gptossmlaattention_pa_kernel(tc, hidden_states, cos, sin, Wkva, bkva, W
         rope_pool = ctx.enter_context(tc.tile_pool(name="rope", bufs=2))
         kk_pool = ctx.enter_context(tc.tile_pool(name="kk", bufs=2))
         v_pool = ctx.enter_context(tc.tile_pool(name="v", bufs=6))
-        psum_xt = ctx.enter_context(tc.psum_pool(name="psum_xt", bufs=2))
         psum_lat = ctx.enter_context(tc.psum_pool(name="psum_lat", bufs=2))
         psum_rope = ctx.enter_context(tc.psum_pool(name="psum_rope", bufs=1))
-        psum_kv = ctx.enter_context(tc.psum_pool(name="psum_kv", bufs=3))
+        psum_turn = ctx.enter_context(tc.psum_pool(name="psum_turn", bufs=5))
 
         bias_rows = const.tile([P, P], BF16)
         nc.vector.memset(bias_rows[:], 0.0)
@@ -73,7 +72,9 @@ def tile_gptossmlaattention_pa_kernel(tc, hidden_states, cos, sin, Wkva, bkva, W
                 out=raw_a[:, kp, :, :].rearrange("p (u e) c -> p u (e c)", e=2), in_=wa_dram[kp]
             )
         hid_raw = [inputs.tile([P, J * HID], BF16, name="hid_raw%d" % g) for g in range(GROUPS)]
-        nc.sync.dma_start(out=hid_raw[0][:], in_=hid_dram[0])
+        for half in range(2):
+            cols = slice(half * J * HID // 2, (half + 1) * J * HID // 2)
+            nc.sync.dma_start(out=hid_raw[0][:, cols], in_=hid_dram[0][:, cols])
         raw_b = inputs.tile([P, PACK, HEADS * (NOPE + VDIM)], BF16)
         half_cols = HALF_HEADS * (NOPE + VDIM)
         for half in range(2):
@@ -92,11 +93,11 @@ def tile_gptossmlaattention_pa_kernel(tc, hidden_states, cos, sin, Wkva, bkva, W
         ident_bf16 = const.tile([P, P], BF16)
         nc.vector.tensor_copy(out=ident_bf16[:], in_=ident_f32[:])
 
-        bias_t_ps = psum_xt.tile([P, P], BF16, tag="xt")
+        bias_t_ps = psum_turn.tile([P, P], BF16, tag="turn")
         nc.tensor.transpose(out=bias_t_ps[:], in_=bias_rows[:], identity=ident_bf16[:])
         lat_bias = const.tile([P, PACK], F32)
         nc.vector.tensor_copy(out=lat_bias[:], in_=bias_t_ps[:, 0:PACK])
-        rope_bias_ps = psum_xt.tile([P, ROPE], F32, tag="xt")
+        rope_bias_ps = psum_turn.tile([P, ROPE], F32, tag="turn")
         nc.tensor.matmul(
             out=rope_bias_ps[:],
             lhsT=ident_bf16[:, BIAS_ROWS - 1 : BIAS_ROWS].to_broadcast([P, P]),
@@ -161,7 +162,7 @@ def tile_gptossmlaattention_pa_kernel(tc, hidden_states, cos, sin, Wkva, bkva, W
         def front(i):
             g, j = divmod(i, J)
             hid_words = hid_raw[g][:].bitcast(F32)
-            xt = psum_xt.tile([P, WORD_BLOCKS, P], F32, tag="xt")
+            xt = psum_turn.tile([P, WORD_BLOCKS, P], F32, tag="turn")
             for q in range(WORD_BLOCKS):
                 w0 = (j * WORD_BLOCKS + q) * P
                 nc.tensor.transpose(out=xt[:, q, :], in_=hid_words[:, w0 : w0 + P], identity=ident_f32[:])
@@ -263,7 +264,7 @@ def tile_gptossmlaattention_pa_kernel(tc, hidden_states, cos, sin, Wkva, bkva, W
                     v_pool.tile([P, HALF_HEADS, J, VDIM], F32, name="v_stage", tag="v_stage") for half in range(2)
                 ]
             lat_codes, lat_scales = lat_q[g]
-            kv_ps = psum_kv.tile([P, KV_CHUNK], F32)
+            kv_ps = psum_turn.tile([P, KV_CHUNK], F32, tag="turn")
             cols = slice(n * KV_CHUNK, (n + 1) * KV_CHUNK)
             nc.tensor.matmul_mx(
                 out=kv_ps[:],

@@ -42,7 +42,7 @@ FLOPS = 2 * SEQ * HID * (RANK + ROPE) + 2 * SEQ * RANK * HEADS * (NOPE + VDIM)
 def tile_gptossmlaattention_pa_kernel(tc, hidden_states, cos, sin, Wkva, bkva, Wkvb, out_0, out_1):
     nc = tc.nc
 
-    hid_dram = hidden_states[0, :, :].rearrange("(p g j) k -> g p (j k)", p=P, j=J)
+    hid_dram = hidden_states[0, :, :].rearrange("(p i) k -> p (i k)", p=P)
     cos_dram = cos[0, :, :].rearrange("(p s) d -> p (s d)", p=P)
     sin_dram = sin[0, :, :].rearrange("(p s) d -> p (s d)", p=P)
     kk_dram = out_0[0, :, :, :].rearrange("h (p g j) d -> g p h (j d)", p=P, j=J)
@@ -58,9 +58,10 @@ def tile_gptossmlaattention_pa_kernel(tc, hidden_states, cos, sin, Wkva, bkva, W
         rope_pool = ctx.enter_context(tc.tile_pool(name="rope", bufs=2))
         kk_pool = ctx.enter_context(tc.tile_pool(name="kk", bufs=2))
         v_pool = ctx.enter_context(tc.tile_pool(name="v", bufs=6))
+        psum_xt = ctx.enter_context(tc.psum_pool(name="psum_xt", bufs=2))
         psum_lat = ctx.enter_context(tc.psum_pool(name="psum_lat", bufs=2))
         psum_rope = ctx.enter_context(tc.psum_pool(name="psum_rope", bufs=1))
-        psum_turn = ctx.enter_context(tc.psum_pool(name="psum_turn", bufs=5))
+        psum_kv = ctx.enter_context(tc.psum_pool(name="psum_kv", bufs=3))
 
         bias_rows = const.tile([P, P], BF16)
         nc.vector.memset(bias_rows[:], 0.0)
@@ -71,42 +72,50 @@ def tile_gptossmlaattention_pa_kernel(tc, hidden_states, cos, sin, Wkva, bkva, W
             nc.sync.dma_start(
                 out=raw_a[:, kp, :, :].rearrange("p (u e) c -> p u (e c)", e=2), in_=wa_dram[kp]
             )
-        hid_raw = [inputs.tile([P, J * HID], BF16, name="hid_raw%d" % g) for g in range(GROUPS)]
-        for half in range(2):
-            cols = slice(half * J * HID // 2, (half + 1) * J * HID // 2)
-            nc.sync.dma_start(out=hid_raw[0][:, cols], in_=hid_dram[0][:, cols])
+        hid_rows = {}
+
+        def load_hidden(first, count):
+            raw = inputs.tile([P, count * HID], BF16, name="hid_raw%d" % first)
+            nc.sync.dma_start(out=raw[:], in_=hid_dram[:, first * HID : (first + count) * HID])
+            for k in range(count):
+                hid_rows[first + k] = raw[:, k * HID : (k + 1) * HID]
+
+        load_hidden(0, J // 2)
+        load_hidden(J // 2, J // 2)
         raw_b = inputs.tile([P, PACK, HEADS * (NOPE + VDIM)], BF16)
         half_cols = HALF_HEADS * (NOPE + VDIM)
         for half in range(2):
             cols = slice(half * half_cols, (half + 1) * half_cols)
             nc.sync.dma_start(out=raw_b[:, :, cols], in_=wb_dram[:, :, cols])
-        nc.sync.dma_start(out=hid_raw[1][:], in_=hid_dram[1])
+        load_hidden(J, J)
         cos_sb = inputs.tile([P, GROUPS, J, ROPE], BF16)
         sin_sb = inputs.tile([P, GROUPS, J, ROPE], BF16)
         nc.sync.dma_start(out=cos_sb[:].rearrange("p g j d -> p (g j d)"), in_=cos_dram)
         nc.sync.dma_start(out=sin_sb[:].rearrange("p g j d -> p (g j d)"), in_=sin_dram)
         for g in range(2, GROUPS):
-            nc.sync.dma_start(out=hid_raw[g][:], in_=hid_dram[g])
+            load_hidden(g * J, J)
 
         ident_f32 = const.tile([P, P], F32)
         make_identity(nc, ident_f32[:])
-        ident_bf16 = const.tile([P, P], BF16)
-        nc.vector.tensor_copy(out=ident_bf16[:], in_=ident_f32[:])
-
-        bias_t_ps = psum_turn.tile([P, P], BF16, tag="turn")
-        nc.tensor.transpose(out=bias_t_ps[:], in_=bias_rows[:], identity=ident_bf16[:])
         lat_bias = const.tile([P, PACK], F32)
-        nc.vector.tensor_copy(out=lat_bias[:], in_=bias_t_ps[:, 0:PACK])
-        rope_bias_ps = psum_turn.tile([P, ROPE], F32, tag="turn")
-        nc.tensor.matmul(
-            out=rope_bias_ps[:],
-            lhsT=ident_bf16[:, BIAS_ROWS - 1 : BIAS_ROWS].to_broadcast([P, P]),
-            rhs=bias_rows[:],
-            start=True,
-            stop=True,
-        )
         rope_bias = const.tile([P, ROPE], F32)
-        nc.vector.tensor_copy(out=rope_bias[:], in_=rope_bias_ps[:])
+
+        def spread_biases():
+            ident_bf16 = const.tile([P, P], BF16)
+            nc.vector.tensor_copy(out=ident_bf16[:], in_=ident_f32[:])
+
+            bias_t_ps = psum_xt.tile([P, P], BF16, tag="xt")
+            nc.tensor.transpose(out=bias_t_ps[:], in_=bias_rows[:], identity=ident_bf16[:])
+            nc.vector.tensor_copy(out=lat_bias[:], in_=bias_t_ps[:, 0:PACK])
+            rope_bias_ps = psum_xt.tile([P, ROPE], F32, tag="xt")
+            nc.tensor.matmul(
+                out=rope_bias_ps[:],
+                lhsT=ident_bf16[:, BIAS_ROWS - 1 : BIAS_ROWS].to_broadcast([P, P]),
+                rhs=bias_rows[:],
+                start=True,
+                stop=True,
+            )
+            nc.vector.tensor_copy(out=rope_bias[:], in_=rope_bias_ps[:])
 
         a_codes = const.tile([P, HID_PASSES, RANK + ROPE], U32, align_bytes=64)
         a_scales = const.tile([P, HID_PASSES, RANK + ROPE], U8, align_bytes=64)
@@ -160,12 +169,10 @@ def tile_gptossmlaattention_pa_kernel(tc, hidden_states, cos, sin, Wkva, bkva, W
         v_stage = {}
 
         def front(i):
-            g, j = divmod(i, J)
-            hid_words = hid_raw[g][:].bitcast(F32)
-            xt = psum_turn.tile([P, WORD_BLOCKS, P], F32, tag="turn")
+            hid_words = hid_rows[i].bitcast(F32)
+            xt = psum_xt.tile([P, WORD_BLOCKS, P], F32, tag="xt")
             for q in range(WORD_BLOCKS):
-                w0 = (j * WORD_BLOCKS + q) * P
-                nc.tensor.transpose(out=xt[:, q, :], in_=hid_words[:, w0 : w0 + P], identity=ident_f32[:])
+                nc.tensor.transpose(out=xt[:, q, :], in_=hid_words[:, q * P : (q + 1) * P], identity=ident_f32[:])
             hid_grouped = work.tile([P, HID_PASSES * P * PACK], BF16, align_bytes=64)
             nc.scalar.copy(
                 out=hid_grouped[:].bitcast(F32).rearrange("p (kp c u) -> p kp c u", kp=HID_PASSES, u=2),
@@ -264,7 +271,7 @@ def tile_gptossmlaattention_pa_kernel(tc, hidden_states, cos, sin, Wkva, bkva, W
                     v_pool.tile([P, HALF_HEADS, J, VDIM], F32, name="v_stage", tag="v_stage") for half in range(2)
                 ]
             lat_codes, lat_scales = lat_q[g]
-            kv_ps = psum_turn.tile([P, KV_CHUNK], F32, tag="turn")
+            kv_ps = psum_kv.tile([P, KV_CHUNK], F32)
             cols = slice(n * KV_CHUNK, (n + 1) * KV_CHUNK)
             nc.tensor.matmul_mx(
                 out=kv_ps[:],
@@ -303,6 +310,8 @@ def tile_gptossmlaattention_pa_kernel(tc, hidden_states, cos, sin, Wkva, bkva, W
                 front(s)
             if s % 2 == 1 and s // 2 < KV_CHUNKS:
                 regroup_b(s // 2)
+            if s == 1:
+                spread_biases()
             if 1 <= s <= TILES:
                 middle(s - 1)
             if s >= GROUP_LAG:

from contextlib import ExitStack

import concourse.mybir as mybir
from concourse.masks import make_identity

F32 = mybir.dt.float32
BF16 = mybir.dt.bfloat16
U32 = mybir.dt.uint32
U8 = mybir.dt.uint8
FP8X4 = mybir.dt.float8_e4m3fn_x4
ADD = mybir.AluOpType.add
MULT = mybir.AluOpType.mult

P = 128
PACK = 4
K_PASS = P * PACK

SEQ = 2048
HID = 1024
HEADS = 8
NOPE = 64
ROPE = 128
VDIM = 128
RANK = 512

HID_PASSES = HID // K_PASS
WORD_BLOCKS = HID // 2 // P
J = 4
GROUPS = SEQ // (P * J)
TILES = GROUPS * J
HALF_HEADS = HEADS // 2
HALF_ROPE = ROPE // 2
KV_CHUNK = 512
KV_CHUNKS = HEADS * (NOPE + VDIM) // KV_CHUNK
BIAS_ROWS = (RANK + ROPE) // P

GROUP_LAG = J

FLOPS = 2 * SEQ * HID * (RANK + ROPE) + 2 * SEQ * RANK * HEADS * (NOPE + VDIM)


def tile_gptossmlaattention_pa_kernel(tc, hidden_states, cos, sin, Wkva, bkva, Wkvb, out_0, out_1):
    nc = tc.nc

    hid_dram = hidden_states[0, :, :].rearrange("(p i) k -> p (i k)", p=P)
    cos_dram = cos[0, :, :].rearrange("(p s) d -> p (s d)", p=P)
    sin_dram = sin[0, :, :].rearrange("(p s) d -> p (s d)", p=P)
    kk_dram = out_0[0, :, :, :].rearrange("h (p g j) d -> g p h (j d)", p=P, j=J)
    v_dram = out_1[0, :, :, :].rearrange("h (p g j) d -> g p h (j d)", p=P, j=J)
    wa_dram = Wkva.rearrange("(kp u p e) c -> kp p u (e c)", kp=HID_PASSES, u=2, p=P, e=2)
    wb_dram = Wkvb.rearrange("(t p) n -> p t n", p=P)

    with ExitStack() as ctx:
        const = ctx.enter_context(tc.tile_pool(name="const", bufs=1))
        inputs = ctx.enter_context(tc.tile_pool(name="inputs", bufs=1))
        wstage = ctx.enter_context(tc.tile_pool(name="wstage", bufs=2))
        work = ctx.enter_context(tc.tile_pool(name="work", bufs=3))
        rope_pool = ctx.enter_context(tc.tile_pool(name="rope", bufs=2))
        kk_pool = ctx.enter_context(tc.tile_pool(name="kk", bufs=2))
        v_pool = ctx.enter_context(tc.tile_pool(name="v", bufs=6))
        psum_xt = ctx.enter_context(tc.psum_pool(name="psum_xt", bufs=2))
        psum_lat = ctx.enter_context(tc.psum_pool(name="psum_lat", bufs=2))
        psum_rope = ctx.enter_context(tc.psum_pool(name="psum_rope", bufs=1))
        psum_kv = ctx.enter_context(tc.psum_pool(name="psum_kv", bufs=3))

        bias_rows = const.tile([P, P], BF16)
        nc.vector.memset(bias_rows[:], 0.0)
        nc.scalar.dma_start(out=bias_rows[0:BIAS_ROWS, :], in_=bkva.rearrange("(r c) -> r c", c=P))

        raw_a = inputs.tile([P, HID_PASSES, PACK, RANK + ROPE], BF16)
        for kp in range(HID_PASSES):
            nc.sync.dma_start(
                out=raw_a[:, kp, :, :].rearrange("p (u e) c -> p u (e c)", e=2), in_=wa_dram[kp]
            )
        hid_rows = {}

        def load_hidden(first, count):
            raw = inputs.tile([P, count * HID], BF16, name="hid_raw%d" % first)
            nc.sync.dma_start(out=raw[:], in_=hid_dram[:, first * HID : (first + count) * HID])
            for k in range(count):
                hid_rows[first + k] = raw[:, k * HID : (k + 1) * HID]

        load_hidden(0, J // 2)
        load_hidden(J // 2, J // 2)
        raw_b = inputs.tile([P, PACK, HEADS * (NOPE + VDIM)], BF16)
        half_cols = HALF_HEADS * (NOPE + VDIM)
        for half in range(2):
            cols = slice(half * half_cols, (half + 1) * half_cols)
            nc.sync.dma_start(out=raw_b[:, :, cols], in_=wb_dram[:, :, cols])
        load_hidden(J, J)
        cos_sb = inputs.tile([P, GROUPS, J, ROPE], BF16)
        sin_sb = inputs.tile([P, GROUPS, J, ROPE], BF16)
        nc.sync.dma_start(out=cos_sb[:].rearrange("p g j d -> p (g j d)"), in_=cos_dram)
        nc.sync.dma_start(out=sin_sb[:].rearrange("p g j d -> p (g j d)"), in_=sin_dram)
        for g in range(2, GROUPS):
            load_hidden(g * J, J)

        ident_f32 = const.tile([P, P], F32)
        make_identity(nc, ident_f32[:])
        lat_bias = const.tile([P, PACK], F32)
        rope_bias = const.tile([P, ROPE], F32)

        def spread_biases():
            ident_bf16 = const.tile([P, P], BF16)
            nc.vector.tensor_copy(out=ident_bf16[:], in_=ident_f32[:])

            bias_t_ps = psum_xt.tile([P, P], BF16, tag="xt")
            nc.tensor.transpose(out=bias_t_ps[:], in_=bias_rows[:], identity=ident_bf16[:])
            nc.vector.tensor_copy(out=lat_bias[:], in_=bias_t_ps[:, 0:PACK])
            rope_bias_ps = psum_xt.tile([P, ROPE], F32, tag="xt")
            nc.tensor.matmul(
                out=rope_bias_ps[:],
                lhsT=ident_bf16[:, BIAS_ROWS - 1 : BIAS_ROWS].to_broadcast([P, P]),
                rhs=bias_rows[:],
                start=True,
                stop=True,
            )
            nc.vector.tensor_copy(out=rope_bias[:], in_=rope_bias_ps[:])

        a_codes = const.tile([P, HID_PASSES, RANK + ROPE], U32, align_bytes=64)
        a_scales = const.tile([P, HID_PASSES, RANK + ROPE], U8, align_bytes=64)
        grouped_a = []
        for kp in range(HID_PASSES):
            grouped = wstage.tile([P, RANK + ROPE, PACK], BF16, align_bytes=64, name="grouped_a", tag="grouped_a")
            nc.vector.tensor_copy(
                out=grouped[:].rearrange("p (c i) t -> p c t i", i=4),
                in_=raw_a[:, kp, :, :].rearrange("p t (c i) -> p c t i", i=4),
            )
            grouped_a.append(grouped)
        for kp in range(HID_PASSES):
            for cols in (slice(0, RANK), slice(RANK, RANK + ROPE)):
                nc.vector.quantize_mx(
                    out=a_codes[:, kp, cols].bitcast(FP8X4),
                    scales=a_scales[:, kp, cols],
                    in_=grouped_a[kp][:, cols, :].rearrange("p c t -> p (c t)"),
                )

        b_codes = const.tile([P, KV_CHUNKS * KV_CHUNK], U32, align_bytes=64)
        b_scales = const.tile([P, KV_CHUNKS * KV_CHUNK], U8, align_bytes=64)
        raw_b_heads = raw_b[:].rearrange("p t (h x) -> p t h x", x=NOPE + VDIM)
        b_sources = [
            raw_b_heads[:, :, 0:HALF_HEADS, NOPE:],
            raw_b_heads[:, :, HALF_HEADS:HEADS, NOPE:],
            raw_b_heads[:, :, :, 0:NOPE],
        ]
        grouped_b = {}

        def regroup_b(n):
            grouped_b[n] = wstage.tile([P, KV_CHUNK, PACK], BF16, align_bytes=64, name="grouped_b", tag="grouped_b")
            copy = nc.scalar.copy if n < 2 else nc.vector.tensor_copy
            copy(
                out=grouped_b[n][:].rearrange("p (h d) t -> p h d t", h=b_sources[n].shape[2]),
                in_=b_sources[n].rearrange("p t h d -> p h d t"),
            )

        def quantise_b(n):
            cols = slice(n * KV_CHUNK, (n + 1) * KV_CHUNK)
            nc.vector.quantize_mx(
                out=b_codes[:, cols].bitcast(FP8X4),
                scales=b_scales[:, cols],
                in_=grouped_b[n][:].rearrange("p c t -> p (c t)"),
            )

        hid_q = {}
        lat_q = {}
        rope_ps = {}
        rope_sb = {}
        kk_stage = {}
        v_stage = {}

        def front(i):
            hid_words = hid_rows[i].bitcast(F32)
            xt = psum_xt.tile([P, WORD_BLOCKS, P], F32, tag="xt")
            for q in range(WORD_BLOCKS):
                nc.tensor.transpose(out=xt[:, q, :], in_=hid_words[:, q * P : (q + 1) * P], identity=ident_f32[:])
            hid_grouped = work.tile([P, HID_PASSES * P * PACK], BF16, align_bytes=64)
            nc.scalar.copy(
                out=hid_grouped[:].bitcast(F32).rearrange("p (kp c u) -> p kp c u", kp=HID_PASSES, u=2),
                in_=xt[:].rearrange("p (kp u) c -> p kp c u", u=2),
            )
            hid_codes = work.tile([P, HID_PASSES, P], U32, align_bytes=64)
            hid_scales = work.tile([P, HID_PASSES, P], U8, align_bytes=64)
            nc.vector.quantize_mx(
                out=hid_codes[:].rearrange("p kp c -> p (kp c)").bitcast(FP8X4),
                scales=hid_scales[:].rearrange("p kp c -> p (kp c)"),
                in_=hid_grouped[:],
            )
            hid_q[i] = (hid_codes, hid_scales)

        def middle(i):
            g, j = divmod(i, J)
            hid_codes, hid_scales = hid_q[i]
            if j == 0:
                rope_ps[g] = psum_rope.tile([P, J, ROPE], F32, name="rope_ps")
                lat_q[g] = (
                    work.tile([P, J, P], U32, align_bytes=64, name="lat_codes"),
                    work.tile([P, J, P], U8, align_bytes=64, name="lat_scales"),
                )
            lat_ps = psum_lat.tile([P, PACK, P], F32)
            for t in range(PACK):
                for kp in range(HID_PASSES):
                    nc.tensor.matmul_mx(
                        out=lat_ps[:, t, :],
                        lhsT=a_codes[:, kp, t * P : (t + 1) * P].bitcast(FP8X4),
                        lhsT_scale=a_scales[:, kp, t * P : (t + 1) * P],
                        rhs=hid_codes[:, kp, :].bitcast(FP8X4),
                        rhs_scale=hid_scales[:, kp, :],
                        start=(kp == 0),
                        stop=(kp == HID_PASSES - 1),
                    )
            for kp in range(HID_PASSES):
                nc.tensor.matmul_mx(
                    out=rope_ps[g][:, j, :],
                    lhsT=hid_codes[:, kp, :].bitcast(FP8X4),
                    lhsT_scale=hid_scales[:, kp, :],
                    rhs=a_codes[:, kp, RANK : RANK + ROPE].bitcast(FP8X4),
                    rhs_scale=a_scales[:, kp, RANK : RANK + ROPE],
                    start=(kp == 0),
                    stop=(kp == HID_PASSES - 1),
                )
            lat_grouped = work.tile([P, P, PACK], BF16, align_bytes=64)
            nc.vector.tensor_tensor(
                out=lat_grouped[:],
                in0=lat_ps[:].rearrange("p t c -> p c t"),
                in1=lat_bias[:].unsqueeze(1).to_broadcast([P, P, PACK]),
                op=ADD,
            )
            lat_codes, lat_scales = lat_q[g]
            nc.vector.quantize_mx(
                out=lat_codes[:, j, :].bitcast(FP8X4),
                scales=lat_scales[:, j, :],
                in_=lat_grouped[:].rearrange("p c t -> p (c t)"),
            )

        def rotate(g, part):
            if part == 0:
                kk_stage[g] = kk_pool.tile([P, HEADS, J, NOPE + ROPE], F32, name="kk_stage")
                rope_sb[g] = (
                    rope_pool.tile([P, J, ROPE], F32, name="k_rope"),
                    rope_pool.tile([P, J, ROPE], F32, name="k_rot"),
                    rope_pool.tile([P, J, ROPE], F32, name="crossed"),
                )
            k_rope, k_rot, crossed = rope_sb[g]
            lo = slice(0, HALF_ROPE)
            hi = slice(HALF_ROPE, ROPE)
            if part == 0:
                nc.vector.tensor_tensor(
                    out=k_rope[:],
                    in0=rope_ps[g][:],
                    in1=rope_bias[:].unsqueeze(1).to_broadcast([P, J, ROPE]),
                    op=ADD,
                )
            if part == 1:
                nc.vector.tensor_tensor(out=k_rot[:], in0=k_rope[:], in1=cos_sb[:, g, :, :], op=MULT)
                nc.vector.scalar_tensor_tensor(
                    out=crossed[:, :, lo], in0=k_rope[:, :, hi], scalar=-1.0, in1=sin_sb[:, g, :, lo], op0=MULT, op1=MULT
                )
                nc.vector.tensor_tensor(out=crossed[:, :, hi], in0=k_rope[:, :, lo], in1=sin_sb[:, g, :, hi], op=MULT)
            if part == 2:
                nc.vector.tensor_tensor(out=k_rot[:], in0=k_rot[:], in1=crossed[:], op=ADD)
            if part >= 2:
                heads = slice((part - 2) * HALF_HEADS, (part - 1) * HALF_HEADS)
                nc.vector.tensor_copy(
                    out=kk_stage[g][:, heads, :, NOPE:],
                    in_=k_rot[:].unsqueeze(1).to_broadcast([P, HALF_HEADS, J, ROPE]),
                )

        def second(g, n, j):
            if n == 0 and j == 0:
                v_stage[g] = [
                    v_pool.tile([P, HALF_HEADS, J, VDIM], F32, name="v_stage", tag="v_stage") for half in range(2)
                ]
            lat_codes, lat_scales = lat_q[g]
            kv_ps = psum_kv.tile([P, KV_CHUNK], F32)
            cols = slice(n * KV_CHUNK, (n + 1) * KV_CHUNK)
            nc.tensor.matmul_mx(
                out=kv_ps[:],
                lhsT=lat_codes[:, j, :].bitcast(FP8X4),
                lhsT_scale=lat_scales[:, j, :],
                rhs=b_codes[:, cols].bitcast(FP8X4),
                rhs_scale=b_scales[:, cols],
                start=True,
                stop=True,
            )
            if n < 2:
                nc.scalar.copy(out=v_stage[g][n][:, :, j, :], in_=kv_ps[:].rearrange("p (h d) -> p h d", d=VDIM))
                if j == J - 1:
                    heads = slice(n * HALF_HEADS, (n + 1) * HALF_HEADS)
                    nc.sync.dma_start(
                        out=v_dram[g, :, heads, :], in_=v_stage[g][n][:].rearrange("p h j d -> p h (j d)")
                    )
            else:
                nc.scalar.copy(out=kk_stage[g][:, :, j, 0:NOPE], in_=kv_ps[:].rearrange("p (h d) -> p h d", d=NOPE))

        def store_kk(g):
            for half in range(2):
                heads = slice(half * HALF_HEADS, (half + 1) * HALF_HEADS)
                nc.sync.dma_start(
                    out=kk_dram[g, :, heads, :], in_=kk_stage[g][:, heads, :, :].rearrange("p h j d -> p h (j d)")
                )

        for s in range(TILES + GROUP_LAG):
            if s % 2 == 0 and 1 <= s // 2 <= KV_CHUNKS:
                quantise_b(s // 2 - 1)
            if s >= GROUP_LAG:
                g, quarter = divmod(s - GROUP_LAG, J)
                for unit in range(KV_CHUNKS * quarter, KV_CHUNKS * (quarter + 1)):
                    second(g, *divmod(unit, J))
            if s < TILES:
                front(s)
            if s % 2 == 1 and s // 2 < KV_CHUNKS:
                regroup_b(s // 2)
            if s == 1:
                spread_biases()
            if 1 <= s <= TILES:
                middle(s - 1)
            if s >= GROUP_LAG:
                rotate(g, quarter)
                if quarter == J - 1:
                    store_kk(g)
